import numpy as np
import ml_dtypes


def mxq(x, axis, fmt="e4m3"):
    dtype, down = {"e4m3": (ml_dtypes.float8_e4m3fn, 7), "e5m2": (ml_dtypes.float8_e5m2, 14)}[fmt]
    v = np.moveaxis(np.asarray(x, np.float32).astype(ml_dtypes.bfloat16).astype(np.float64), axis, -1)
    blocks = v.reshape(v.shape[:-1] + (-1, 32))
    amax = np.abs(blocks).max(-1, keepdims=True)
    byte = np.maximum(np.where(amax > 0, np.frexp(amax)[1] - 1 + 127, 0) - down, 1)
    scale = np.exp2(byte - 127.0)
    codes = (blocks / scale).astype(np.float32).astype(dtype).astype(np.float64)
    return np.moveaxis((codes * scale).reshape(v.shape), -1, axis)


WIDE = False


def mx_kscale(k):
    if not WIDE:
        return np.ones(k)
    levels = np.array([10, -10, 5, -5, 0])
    a = np.random.permutation(np.resize(levels, k // 512 * 4)).reshape(k // 512, 4)
    idx = np.arange(k)
    return np.exp2(a[idx // 512, idx % 128 // 32])


BF16 = ml_dtypes.bfloat16


def bf(x):
    return np.asarray(x, np.float32).astype(BF16)


def f64(x):
    return np.asarray(x).astype(np.float64)


E2M1 = np.array([0.0, 0.5, 1.0, 1.5, 2.0, 3.0, 4.0, 6.0, -0.0, -0.5, -1.0, -1.5, -2.0, -3.0, -4.0, -6.0])


def pack_weight(w, fmt):
    k, n = w.shape
    w = f64(bf(w)).reshape(k // 32, 32, n)
    amax = np.abs(w).max(1)
    if fmt == "e4m3":
        byte = np.frexp(amax)[1] - 1 + 127 - 7
    else:
        mant, ex = np.frexp(amax / 6.0)
        byte = np.where(mant > 0.5, ex, ex - 1) + 127
    byte = np.clip(np.where(amax > 0, byte, 1), 1, 254)
    scaled = (w * np.exp2(127.0 - byte)[:, None, :]).reshape(k, n).astype(np.float32)
    by_word = np.ascontiguousarray(scaled.reshape(k // 512, 128, 4, n).transpose(0, 1, 3, 2))
    if fmt == "e4m3":
        words = by_word.astype(ml_dtypes.float8_e4m3fn).view(np.uint8)
    else:
        c = by_word.astype(ml_dtypes.float4_e2m1fn).view(np.uint8) & 0xF
        words = c[..., 0::2] | (c[..., 1::2] << 4)
    return np.ascontiguousarray(words), np.ascontiguousarray(byte.astype(np.uint8).reshape(k // 512, 16, n))


def unpack_weight(words, scales, fmt):
    g, p, n, _ = words.shape
    if fmt == "e4m3":
        vals = np.ascontiguousarray(words).view(ml_dtypes.float8_e4m3fn).astype(np.float64)
    else:
        nib = np.empty((g, p, n, 4), np.uint8)
        nib[..., 0::2] = words & 0xF
        nib[..., 1::2] = words >> 4
        vals = E2M1[nib]
    vals = vals * np.repeat(np.exp2(scales.astype(np.float64) - 127.0), 8, axis=1)[..., None]
    return vals.transpose(0, 1, 3, 2).reshape(g * 512, n)

def pack4(w):
    words, scales = pack_weight(w, "e2m1")
    return words.reshape(words.shape[0], 128, -1), scales


def unpack4(words, scales):
    return unpack_weight(words.reshape(words.shape[0], 128, -1, 2), scales, "e2m1")


B, C, D, T, H, W, P = 1, 16384, 128, 8, 8, 8, 2
N = T * H * W
NP = T * (H // P) * (W // P)


def conv1x1(wq, b, xq):
    return ((wq @ xq) + b[None, :, None]).reshape(B, D, T, H, W)


def maxpool(v):
    return v.reshape(B, D, T, H // P, P, W // P, P).max(axis=(4, 6))


def setup_inputs():
    s = mx_kscale(C)
    a = 1.0 / np.sqrt(C) / s[None, :]
    x = bf(np.random.standard_normal((B, C, T, H, W)) * s[None, :, None, None, None])
    g_w_words, g_w_scales = pack4(np.ascontiguousarray((np.random.standard_normal((D, C)) * 0.15 * a).T))
    g_b = bf(np.random.standard_normal(D) * 0.03)
    theta_w_words, theta_w_scales = pack4(np.ascontiguousarray((np.random.standard_normal((D, C)) * 2.0 * a).T))
    theta_b = bf(np.random.standard_normal(D) * 0.2)
    phi_w_words, phi_w_scales = pack4(np.ascontiguousarray((np.random.standard_normal((D, C)) * a).T))
    phi_b = bf(np.random.standard_normal(D) * 0.1)
    return {"x": x,
            "g_w_words": g_w_words,
            "g_w_scales": g_w_scales,
            "g_b": g_b,
            "theta_w_words": theta_w_words,
            "theta_w_scales": theta_w_scales,
            "theta_b": theta_b,
            "phi_w_words": phi_w_words,
            "phi_w_scales": phi_w_scales,
            "phi_b": phi_b}


def reference(x, g_w_words, g_w_scales, g_b, theta_w_words, theta_w_scales, theta_b, phi_w_words, phi_w_scales, phi_b):
    xq = mxq(f64(x).reshape(B, C, N), 1, "e4m3")
    g_x = maxpool(conv1x1(unpack4(g_w_words, g_w_scales).T, f64(g_b), xq)).reshape(B, D, NP)
    theta_x = conv1x1(unpack4(theta_w_words, theta_w_scales).T, f64(theta_b), xq).reshape(B, D, N)
    phi_x = maxpool(conv1x1(unpack4(phi_w_words, phi_w_scales).T, f64(phi_b), xq)).reshape(B, D, NP)
    return g_x, theta_x, phi_x

@@ -1,0 +1,154 @@
+from contextlib import ExitStack
+
+import concourse.mybir as mybir
+
+BF16 = mybir.dt.bfloat16
+F32 = mybir.dt.float32
+I32 = mybir.dt.int32
+U8 = mybir.dt.uint8
+U32 = mybir.dt.uint32
+FP8X4 = mybir.dt.float8_e4m3fn_x4
+FP4X4 = mybir.dt.float4_e2m1fn_x4
+IDENTITY = mybir.ActivationFunctionType.Identity
+
+P = 128
+PACK = 4
+K_PASS = P * PACK
+C = 16384
+D = 128
+FRAMES, HEIGHT, WIDTH = 8, 8, 8
+N = FRAMES * HEIGHT * WIDTH
+PASSES = C // K_PASS
+CHUNK = 4
+QUADRANTS = 4
+VECTOR_COLS = 336
+RUN = 4
+
+FLOPS = 2 * 3 * D * C * N
+
+
+def tile_nonlocalblocknd_pa_k_kernel(
+    tc,
+    x,
+    g_w_words,
+    g_w_scales,
+    g_b,
+    theta_w_words,
+    theta_w_scales,
+    theta_b,
+    phi_w_words,
+    phi_w_scales,
+    phi_b,
+    out_0,
+    out_1,
+    out_2,
+):
+    nc = tc.nc
+    convs = ("g", "phi", "theta")
+    words_in = {"g": g_w_words, "phi": phi_w_words, "theta": theta_w_words}
+    scales_in = {"g": g_w_scales, "phi": phi_w_scales, "theta": theta_w_scales}
+    bias_in = {"g": g_b, "phi": phi_b, "theta": theta_b}
+
+    x_rows = x[0].rearrange("(c p j) t h w -> c p j (t h w)", p=P, j=PACK)
+
+    with ExitStack() as ctx:
+        ctx.enter_context(tc.manual_schedule())
+        resident = ctx.enter_context(tc.tile_pool(name="resident", bufs=1))
+        stage = ctx.enter_context(tc.tile_pool(name="stage", bufs=3))
+        quantised = ctx.enter_context(tc.tile_pool(name="quantised", bufs=4))
+        psum = ctx.enter_context(tc.psum_pool(name="psum", bufs=1))
+
+        x_raw = [resident.tile([P, PACK, N], BF16, name="x_raw%d" % c) for c in range(PASSES)]
+        words = {
+            v: [
+                resident.tile([P, CHUNK, 2 * D], U8, name="words_%s%d" % (v, i), align_bytes=64)
+                for i in range(PASSES // CHUNK)
+            ]
+            for v in convs
+        }
+        planes = {v: resident.tile([P, PASSES, D], U8, name="planes_%s" % v, align_bytes=64) for v in convs}
+        bias_bf16 = {v: resident.tile([P, 1], BF16, name="bias_bf16_%s" % v) for v in convs}
+        bias = {v: resident.tile([P, 1], F32, name="bias_%s" % v) for v in convs}
+        acc = {v: psum.tile([D, N], F32, name="acc_%s" % v) for v in convs}
+
+        def load_x(c):
+            nc.sync.dma_start(out=x_raw[c][:], in_=x_rows[c])
+
+        def load_words(i):
+            for v in convs:
+                nc.sync.dma_start(
+                    out=words[v][i][:].bitcast(I32),
+                    in_=words_in[v][i * CHUNK : (i + 1) * CHUNK].bitcast(I32).rearrange("c p b -> p c b"),
+                )
+
+        def load_scales(v):
+            rows = scales_in[v].bitcast(I32).rearrange("c (q r) n -> r q c n", r=PACK)
+            for r in range(PACK):
+                nc.sync.dma_start(out=planes[v][r : P : P // QUADRANTS].bitcast(I32), in_=rows[r])
+
+        for v in convs:
+            nc.vector.memset(planes[v][:].bitcast(I32), 0)
+        with nc.allow_non_contiguous_dma(reason="one bias value to a partition, 128 values"):
+            for v in convs:
+                nc.scalar.dma_start(out=bias_bf16[v][:], in_=bias_in[v].rearrange("(d o) -> d o", o=1))
+        load_x(0)
+        for v in convs:
+            load_scales(v)
+        for c in range(PASSES):
+            if c % CHUNK == 0:
+                load_words(c // CHUNK)
+            if c > 0:
+                load_x(c)
+        for v in convs:
+            nc.scalar.activation(out=bias[v][:], in_=bias_bf16[v][:], func=IDENTITY)
+
+        grouped = {}
+
+        def regroup(c):
+            grouped[c] = stage.tile([P, N, PACK], BF16, name="grouped", tag="grouped", align_bytes=64)
+            dst = grouped[c][:].rearrange("p (m i) j -> p m j i", i=RUN)
+            src = x_raw[c][:].rearrange("p j (m i) -> p m j i", i=RUN)
+            split = VECTOR_COLS // RUN
+            nc.vector.tensor_copy(out=dst[:, :split], in_=src[:, :split])
+            nc.scalar.copy(out=dst[:, split:], in_=src[:, split:])
+
+        def quantise_and_multiply(c):
+            codes = quantised.tile([P, N], U32, name="codes", tag="codes", align_bytes=64)
+            x_scales = quantised.tile([P, N], U8, name="x_scales", tag="x_scales", align_bytes=64)
+            nc.vector.quantize_mx(
+                out=codes[:].bitcast(FP8X4),
+                scales=x_scales[:],
+                in_=grouped[c][:].rearrange("p n j -> p (n j)"),
+            )
+            for v in convs:
+                nc.tensor.matmul_mx(
+                    out=acc[v][:],
+                    lhsT=words[v][c // CHUNK][:, c % CHUNK, :].bitcast(FP4X4),
+                    lhsT_scale=planes[v][:, c, :],
+                    rhs=codes[:].bitcast(FP8X4),
+                    rhs_scale=x_scales[:],
+                    start=(c == 0),
+                    stop=(c == PASSES - 1),
+                )
+
+        regroup(0)
+        for c in range(PASSES):
+            if c + 1 < PASSES:
+                regroup(c + 1)
+            quantise_and_multiply(c)
+
+        biased = {v: resident.tile([D, N], F32, name="biased_%s" % v) for v in convs}
+        nc.scalar.activation(out=biased["g"][:], in_=acc["g"][:], func=IDENTITY, bias=bias["g"][:])
+        nc.vector.tensor_scalar_add(out=biased["phi"][:], in0=acc["phi"][:], scalar1=bias["phi"][:])
+        nc.scalar.activation(out=biased["theta"][:], in_=acc["theta"][:], func=IDENTITY, bias=bias["theta"][:])
+        nc.sync.dma_start(out=out_1[0], in_=biased["theta"][:])
+        for v, out in (("g", out_0), ("phi", out_2)):
+            by_row = biased[v][:].rearrange("d (a e w) -> d a e w", e=2, w=WIDTH)
+            tall = resident.tile([D, N // 2], F32, name="tall_%s" % v)
+            nc.vector.tensor_max(
+                out=tall[:].rearrange("d (a w) -> d a w", w=WIDTH), in0=by_row[:, :, 0, :], in1=by_row[:, :, 1, :]
+            )
+            pairs = tall[:].rearrange("d (m e) -> d m e", e=2)
+            pooled = resident.tile([D, N // 4], F32, name="pooled_%s" % v)
+            nc.vector.tensor_max(out=pooled[:], in0=pairs[:, :, 0], in1=pairs[:, :, 1])
+            nc.sync.dma_start(out=out[0], in_=pooled[:])

@@ -21,7 +21,7 @@ N = FRAMES * HEIGHT * WIDTH
 PASSES = C // K_PASS
 CHUNK = 4
 QUADRANTS = 4
-VECTOR_COLS = 336
+VECTOR_COLS = 256
 RUN = 4
 
 FLOPS = 2 * 3 * D * C * N

@@ -20,6 +20,7 @@ FRAMES, HEIGHT, WIDTH = 8, 8, 8
 N = FRAMES * HEIGHT * WIDTH
 PASSES = C // K_PASS
 CHUNK = 4
+QUANTISED = 16
 QUADRANTS = 4
 VECTOR_COLS = 256
 RUN = 4
@@ -55,7 +56,7 @@ def tile_nonlocalblocknd_pa_k_kernel(
         ctx.enter_context(tc.manual_schedule())
         resident = ctx.enter_context(tc.tile_pool(name="resident", bufs=1))
         stage = ctx.enter_context(tc.tile_pool(name="stage", bufs=3))
-        quantised = ctx.enter_context(tc.tile_pool(name="quantised", bufs=4))
+        quantised = ctx.enter_context(tc.tile_pool(name="quantised", bufs=QUANTISED))
         psum = ctx.enter_context(tc.psum_pool(name="psum", bufs=1))
 
         x_raw = [resident.tile([P, PACK, N], BF16, name="x_raw%d" % c) for c in range(PASSES)]
@@ -81,24 +82,25 @@ def tile_nonlocalblocknd_pa_k_kernel(
                     in_=words_in[v][i * CHUNK : (i + 1) * CHUNK].bitcast(I32).rearrange("c p b -> p c b"),
                 )
 
-        def load_scales(v):
+        def load_scales(v, r):
             rows = scales_in[v].bitcast(I32).rearrange("c (q r) n -> r q c n", r=PACK)
-            for r in range(PACK):
-                nc.sync.dma_start(out=planes[v][r : P : P // QUADRANTS].bitcast(I32), in_=rows[r])
+            nc.sync.dma_start(out=planes[v][r : P : P // QUADRANTS].bitcast(I32), in_=rows[r])
 
         for v in convs:
             nc.vector.memset(planes[v][:].bitcast(I32), 0)
         with nc.allow_non_contiguous_dma(reason="one bias value to a partition, 128 values"):
             for v in convs:
                 nc.scalar.dma_start(out=bias_bf16[v][:], in_=bias_in[v].rearrange("(d o) -> d o", o=1))
+        scale_loads = [(v, r) for v in convs for r in range(PACK)]
         load_x(0)
-        for v in convs:
-            load_scales(v)
-        for c in range(PASSES):
+        load_x(1)
+        load_words(0)
+        for c in range(2, PASSES):
             if c % CHUNK == 0:
                 load_words(c // CHUNK)
-            if c > 0:
-                load_x(c)
+            load_x(c)
+            if c - 2 < len(scale_loads):
+                load_scales(*scale_loads[c - 2])
         for v in convs:
             nc.scalar.activation(out=bias[v][:], in_=bias_bf16[v][:], func=IDENTITY)
 

@@ -23,6 +23,7 @@ CHUNK = 4
 QUANTISED = 16
 QUADRANTS = 4
 VECTOR_COLS = 256
+VECTOR_COLS_LAST = 320
 RUN = 4
 
 FLOPS = 2 * 3 * D * C * N
@@ -60,13 +61,7 @@ def tile_nonlocalblocknd_pa_k_kernel(
         psum = ctx.enter_context(tc.psum_pool(name="psum", bufs=1))
 
         x_raw = [resident.tile([P, PACK, N], BF16, name="x_raw%d" % c) for c in range(PASSES)]
-        words = {
-            v: [
-                resident.tile([P, CHUNK, 2 * D], U8, name="words_%s%d" % (v, i), align_bytes=64)
-                for i in range(PASSES // CHUNK)
-            ]
-            for v in convs
-        }
+        words = {v: resident.tile([P, PASSES, 2 * D], U8, name="words_%s" % v, align_bytes=64) for v in convs}
         planes = {v: resident.tile([P, PASSES, D], U8, name="planes_%s" % v, align_bytes=64) for v in convs}
         bias_bf16 = {v: resident.tile([P, 1], BF16, name="bias_bf16_%s" % v) for v in convs}
         bias = {v: resident.tile([P, 1], F32, name="bias_%s" % v) for v in convs}
@@ -75,12 +70,12 @@ def tile_nonlocalblocknd_pa_k_kernel(
         def load_x(c):
             nc.sync.dma_start(out=x_raw[c][:], in_=x_rows[c])
 
-        def load_words(i):
-            for v in convs:
-                nc.sync.dma_start(
-                    out=words[v][i][:].bitcast(I32),
-                    in_=words_in[v][i * CHUNK : (i + 1) * CHUNK].bitcast(I32).rearrange("c p b -> p c b"),
-                )
+        def load_words(v, first):
+            passes = slice(first, first + CHUNK)
+            nc.sync.dma_start(
+                out=words[v][:, passes].bitcast(I32),
+                in_=words_in[v][passes].bitcast(I32).rearrange("c p b -> p c b"),
+            )
 
         def load_scales(v, r):
             rows = scales_in[v].bitcast(I32).rearrange("c (q r) n -> r q c n", r=PACK)
@@ -92,14 +87,11 @@ def tile_nonlocalblocknd_pa_k_kernel(
             for v in convs:
                 nc.scalar.dma_start(out=bias_bf16[v][:], in_=bias_in[v].rearrange("(d o) -> d o", o=1))
         scale_loads = [(v, r) for v in convs for r in range(PACK)]
-        load_x(0)
-        load_x(1)
-        load_words(0)
-        for c in range(2, PASSES):
-            if c % CHUNK == 0:
-                load_words(c // CHUNK)
+        for c in range(PASSES):
             load_x(c)
-            if c - 2 < len(scale_loads):
+            if c % CHUNK > 0:
+                load_words(convs[c % CHUNK - 1], c - c % CHUNK)
+            if 2 <= c < 2 + len(scale_loads):
                 load_scales(*scale_loads[c - 2])
         for v in convs:
             nc.scalar.activation(out=bias[v][:], in_=bias_bf16[v][:], func=IDENTITY)
@@ -110,34 +102,52 @@ def tile_nonlocalblocknd_pa_k_kernel(
             grouped[c] = stage.tile([P, N, PACK], BF16, name="grouped", tag="grouped", align_bytes=64)
             dst = grouped[c][:].rearrange("p (m i) j -> p m j i", i=RUN)
             src = x_raw[c][:].rearrange("p j (m i) -> p m j i", i=RUN)
-            split = VECTOR_COLS // RUN
+            split = (VECTOR_COLS if c < PASSES - 1 else VECTOR_COLS_LAST) // RUN
             nc.vector.tensor_copy(out=dst[:, :split], in_=src[:, :split])
             nc.scalar.copy(out=dst[:, split:], in_=src[:, split:])
 
-        def quantise_and_multiply(c):
-            codes = quantised.tile([P, N], U32, name="codes", tag="codes", align_bytes=64)
-            x_scales = quantised.tile([P, N], U8, name="x_scales", tag="x_scales", align_bytes=64)
+        codes, x_scales = {}, {}
+
+        def quantise(c):
+            codes[c] = quantised.tile([P, N], U32, name="codes", tag="codes", align_bytes=64)
+            x_scales[c] = quantised.tile([P, N], U8, name="x_scales", tag="x_scales", align_bytes=64)
             nc.vector.quantize_mx(
-                out=codes[:].bitcast(FP8X4),
-                scales=x_scales[:],
+                out=codes[c][:].bitcast(FP8X4),
+                scales=x_scales[c][:],
                 in_=grouped[c][:].rearrange("p n j -> p (n j)"),
             )
-            for v in convs:
-                nc.tensor.matmul_mx(
-                    out=acc[v][:],
-                    lhsT=words[v][c // CHUNK][:, c % CHUNK, :].bitcast(FP4X4),
-                    lhsT_scale=planes[v][:, c, :],
-                    rhs=codes[:].bitcast(FP8X4),
-                    rhs_scale=x_scales[:],
-                    start=(c == 0),
-                    stop=(c == PASSES - 1),
-                )
+
+        def multiply(v, c):
+            nc.tensor.matmul_mx(
+                out=acc[v][:],
+                lhsT=words[v][:, c, :].bitcast(FP4X4),
+                lhsT_scale=planes[v][:, c, :],
+                rhs=codes[c][:].bitcast(FP8X4),
+                rhs_scale=x_scales[c][:],
+                start=(c == 0),
+                stop=(c == PASSES - 1),
+            )
+
+        def multiply_after_quantise(c):
+            if c == PASSES - 1:
+                for i, v in enumerate(convs):
+                    for late in range(c - i, c):
+                        multiply(v, late)
+                for v in convs:
+                    multiply(v, c)
+            else:
+                for i, v in enumerate(convs):
+                    if c >= i:
+                        multiply(v, c - i)
 
         regroup(0)
         for c in range(PASSES):
-            if c + 1 < PASSES:
+            if c + 1 < PASSES - 1:
                 regroup(c + 1)
-            quantise_and_multiply(c)
+            quantise(c)
+            multiply_after_quantise(c)
+            if c + 1 == PASSES - 1:
+                regroup(c + 1)
 
         biased = {v: resident.tile([D, N], F32, name="biased_%s" % v) for v in convs}
         nc.scalar.activation(out=biased["g"][:], in_=acc["g"][:], func=IDENTITY, bias=bias["g"][:])

@@ -23,7 +23,8 @@ CHUNK = 4
 QUANTISED = 16
 QUADRANTS = 4
 VECTOR_COLS = 256
-VECTOR_COLS_LAST = 320
+TAIL = 2
+VECTOR_COLS_LAST = 160
 RUN = 4
 
 FLOPS = 2 * 3 * D * C * N
@@ -96,26 +97,33 @@ def tile_nonlocalblocknd_pa_k_kernel(
         for v in convs:
             nc.scalar.activation(out=bias[v][:], in_=bias_bf16[v][:], func=IDENTITY)
 
+        def parts(c):
+            if c < PASSES - 1:
+                return [(0, VECTOR_COLS, N)]
+            return [(h, h + VECTOR_COLS_LAST, h + N // 2) for h in (0, N // 2)]
+
         grouped = {}
 
         def regroup(c):
             grouped[c] = stage.tile([P, N, PACK], BF16, name="grouped", tag="grouped", align_bytes=64)
             dst = grouped[c][:].rearrange("p (m i) j -> p m j i", i=RUN)
             src = x_raw[c][:].rearrange("p j (m i) -> p m j i", i=RUN)
-            split = (VECTOR_COLS if c < PASSES - 1 else VECTOR_COLS_LAST) // RUN
-            nc.vector.tensor_copy(out=dst[:, :split], in_=src[:, :split])
-            nc.scalar.copy(out=dst[:, split:], in_=src[:, split:])
+            for first, split, end in parts(c):
+                vector_share, scalar_share = slice(first // RUN, split // RUN), slice(split // RUN, end // RUN)
+                nc.vector.tensor_copy(out=dst[:, vector_share], in_=src[:, vector_share])
+                nc.scalar.copy(out=dst[:, scalar_share], in_=src[:, scalar_share])
 
         codes, x_scales = {}, {}
 
         def quantise(c):
             codes[c] = quantised.tile([P, N], U32, name="codes", tag="codes", align_bytes=64)
             x_scales[c] = quantised.tile([P, N], U8, name="x_scales", tag="x_scales", align_bytes=64)
-            nc.vector.quantize_mx(
-                out=codes[c][:].bitcast(FP8X4),
-                scales=x_scales[c][:],
-                in_=grouped[c][:].rearrange("p n j -> p (n j)"),
-            )
+            for first, split, end in parts(c):
+                nc.vector.quantize_mx(
+                    out=codes[c][:, first:end].bitcast(FP8X4),
+                    scales=x_scales[c][:, first:end],
+                    in_=grouped[c][:, first:end].rearrange("p n j -> p (n j)"),
+                )
 
         def multiply(v, c):
             nc.tensor.matmul_mx(
@@ -128,39 +136,48 @@ def tile_nonlocalblocknd_pa_k_kernel(
                 stop=(c == PASSES - 1),
             )
 
+        done = {v: 0 for v in convs}
+
+        def multiply_up_to(v, c):
+            for late in range(done[v], c + 1):
+                multiply(v, late)
+            done[v] = max(done[v], c + 1)
+
         def multiply_after_quantise(c):
-            if c == PASSES - 1:
-                for i, v in enumerate(convs):
-                    for late in range(c - i, c):
-                        multiply(v, late)
-                for v in convs:
-                    multiply(v, c)
+            if c < PASSES - 1:
+                multiply_up_to("theta", min(c - 2, PASSES - CHUNK - 1))
+                multiply_up_to("phi", c - 1)
             else:
-                for i, v in enumerate(convs):
-                    if c >= i:
-                        multiply(v, c - i)
+                multiply_up_to("theta", c - 1)
+            multiply_up_to("g", c)
+            if c >= PASSES - 2:
+                multiply_up_to("phi", c)
+            if c == PASSES - 1:
+                multiply_up_to("theta", c)
 
         regroup(0)
         for c in range(PASSES):
-            if c + 1 < PASSES - 1:
+            early = c + 1 < PASSES - TAIL
+            if early:
                 regroup(c + 1)
             quantise(c)
             multiply_after_quantise(c)
-            if c + 1 == PASSES - 1:
+            if not early and c + 1 < PASSES:
                 regroup(c + 1)
 
-        biased = {v: resident.tile([D, N], F32, name="biased_%s" % v) for v in convs}
-        nc.scalar.activation(out=biased["g"][:], in_=acc["g"][:], func=IDENTITY, bias=bias["g"][:])
-        nc.vector.tensor_scalar_add(out=biased["phi"][:], in0=acc["phi"][:], scalar1=bias["phi"][:])
-        nc.scalar.activation(out=biased["theta"][:], in_=acc["theta"][:], func=IDENTITY, bias=bias["theta"][:])
-        nc.sync.dma_start(out=out_1[0], in_=biased["theta"][:])
-        for v, out in (("g", out_0), ("phi", out_2)):
-            by_row = biased[v][:].rearrange("d (a e w) -> d a e w", e=2, w=WIDTH)
-            tall = resident.tile([D, N // 2], F32, name="tall_%s" % v)
-            nc.vector.tensor_max(
-                out=tall[:].rearrange("d (a w) -> d a w", w=WIDTH), in0=by_row[:, :, 0, :], in1=by_row[:, :, 1, :]
+        pooled = {}
+        for v in ("g", "phi"):
+            pooled[v] = resident.tile([D, N // 4], F32, name="pooled_%s" % v)
+            nc.vector.tensor_reduce(
+                out=pooled[v][:].rearrange("d (a b) -> d a b", b=WIDTH // 2),
+                in_=acc[v][:].rearrange("d (a e b f) -> d a b e f", e=2, b=WIDTH // 2, f=2),
+                axis=mybir.AxisListType.XY,
+                op=mybir.AluOpType.max,
             )
-            pairs = tall[:].rearrange("d (m e) -> d m e", e=2)
-            pooled = resident.tile([D, N // 4], F32, name="pooled_%s" % v)
-            nc.vector.tensor_max(out=pooled[:], in0=pairs[:, :, 0], in1=pairs[:, :, 1])
-            nc.sync.dma_start(out=out[0], in_=pooled[:])
+        theta = resident.tile([D, N], F32, name="theta")
+        nc.scalar.activation(out=theta[:], in_=acc["theta"][:], func=IDENTITY, bias=bias["theta"][:])
+        nc.sync.dma_start(out=out_1[0], in_=theta[:])
+        for v, out in (("g", out_0), ("phi", out_2)):
+            biased = resident.tile([D, N // 4], F32, name="biased_%s" % v)
+            nc.scalar.activation(out=biased[:], in_=pooled[v][:], func=IDENTITY, bias=bias[v][:])
+            nc.sync.dma_start(out=out[0], in_=biased[:])

@@ -25,7 +25,7 @@ QUADRANTS = 4
 VECTOR_COLS = 256
 TAIL = 2
 VECTOR_COLS_LAST = 160
-RUN = 4
+RUN = 8
 
 FLOPS = 2 * 3 * D * C * N
 

from contextlib import ExitStack

import concourse.mybir as mybir

BF16 = mybir.dt.bfloat16
F32 = mybir.dt.float32
I32 = mybir.dt.int32
U8 = mybir.dt.uint8
U32 = mybir.dt.uint32
FP8X4 = mybir.dt.float8_e4m3fn_x4
FP4X4 = mybir.dt.float4_e2m1fn_x4
IDENTITY = mybir.ActivationFunctionType.Identity

P = 128
PACK = 4
K_PASS = P * PACK
C = 16384
D = 128
FRAMES, HEIGHT, WIDTH = 8, 8, 8
N = FRAMES * HEIGHT * WIDTH
PASSES = C // K_PASS
CHUNK = 4
QUANTISED = 16
QUADRANTS = 4
VECTOR_COLS = 256
TAIL = 2
VECTOR_COLS_LAST = 160
RUN = 8

FLOPS = 2 * 3 * D * C * N


def tile_nonlocalblocknd_pa_k_kernel(
    tc,
    x,
    g_w_words,
    g_w_scales,
    g_b,
    theta_w_words,
    theta_w_scales,
    theta_b,
    phi_w_words,
    phi_w_scales,
    phi_b,
    out_0,
    out_1,
    out_2,
):
    nc = tc.nc
    convs = ("g", "phi", "theta")
    words_in = {"g": g_w_words, "phi": phi_w_words, "theta": theta_w_words}
    scales_in = {"g": g_w_scales, "phi": phi_w_scales, "theta": theta_w_scales}
    bias_in = {"g": g_b, "phi": phi_b, "theta": theta_b}

    x_rows = x[0].rearrange("(c p j) t h w -> c p j (t h w)", p=P, j=PACK)

    with ExitStack() as ctx:
        ctx.enter_context(tc.manual_schedule())
        resident = ctx.enter_context(tc.tile_pool(name="resident", bufs=1))
        stage = ctx.enter_context(tc.tile_pool(name="stage", bufs=3))
        quantised = ctx.enter_context(tc.tile_pool(name="quantised", bufs=QUANTISED))
        psum = ctx.enter_context(tc.psum_pool(name="psum", bufs=1))

        x_raw = [resident.tile([P, PACK, N], BF16, name="x_raw%d" % c) for c in range(PASSES)]
        words = {v: resident.tile([P, PASSES, 2 * D], U8, name="words_%s" % v, align_bytes=64) for v in convs}
        planes = {v: resident.tile([P, PASSES, D], U8, name="planes_%s" % v, align_bytes=64) for v in convs}
        bias_bf16 = {v: resident.tile([P, 1], BF16, name="bias_bf16_%s" % v) for v in convs}
        bias = {v: resident.tile([P, 1], F32, name="bias_%s" % v) for v in convs}
        acc = {v: psum.tile([D, N], F32, name="acc_%s" % v) for v in convs}

        def load_x(c):
            nc.sync.dma_start(out=x_raw[c][:], in_=x_rows[c])

        def load_words(v, first):
            passes = slice(first, first + CHUNK)
            nc.sync.dma_start(
                out=words[v][:, passes].bitcast(I32),
                in_=words_in[v][passes].bitcast(I32).rearrange("c p b -> p c b"),
            )

        def load_scales(v, r):
            rows = scales_in[v].bitcast(I32).rearrange("c (q r) n -> r q c n", r=PACK)
            nc.sync.dma_start(out=planes[v][r : P : P // QUADRANTS].bitcast(I32), in_=rows[r])

        for v in convs:
            nc.vector.memset(planes[v][:].bitcast(I32), 0)
        with nc.allow_non_contiguous_dma(reason="one bias value to a partition, 128 values"):
            for v in convs:
                nc.scalar.dma_start(out=bias_bf16[v][:], in_=bias_in[v].rearrange("(d o) -> d o", o=1))
        scale_loads = [(v, r) for v in convs for r in range(PACK)]
        for c in range(PASSES):
            load_x(c)
            if c % CHUNK > 0:
                load_words(convs[c % CHUNK - 1], c - c % CHUNK)
            if 2 <= c < 2 + len(scale_loads):
                load_scales(*scale_loads[c - 2])
        for v in convs:
            nc.scalar.activation(out=bias[v][:], in_=bias_bf16[v][:], func=IDENTITY)

        def parts(c):
            if c < PASSES - 1:
                return [(0, VECTOR_COLS, N)]
            return [(h, h + VECTOR_COLS_LAST, h + N // 2) for h in (0, N // 2)]

        grouped = {}

        def regroup(c):
            grouped[c] = stage.tile([P, N, PACK], BF16, name="grouped", tag="grouped", align_bytes=64)
            dst = grouped[c][:].rearrange("p (m i) j -> p m j i", i=RUN)
            src = x_raw[c][:].rearrange("p j (m i) -> p m j i", i=RUN)
            for first, split, end in parts(c):
                vector_share, scalar_share = slice(first // RUN, split // RUN), slice(split // RUN, end // RUN)
                nc.vector.tensor_copy(out=dst[:, vector_share], in_=src[:, vector_share])
                nc.scalar.copy(out=dst[:, scalar_share], in_=src[:, scalar_share])

        codes, x_scales = {}, {}

        def quantise(c):
            codes[c] = quantised.tile([P, N], U32, name="codes", tag="codes", align_bytes=64)
            x_scales[c] = quantised.tile([P, N], U8, name="x_scales", tag="x_scales", align_bytes=64)
            for first, split, end in parts(c):
                nc.vector.quantize_mx(
                    out=codes[c][:, first:end].bitcast(FP8X4),
                    scales=x_scales[c][:, first:end],
                    in_=grouped[c][:, first:end].rearrange("p n j -> p (n j)"),
                )

        def multiply(v, c):
            nc.tensor.matmul_mx(
                out=acc[v][:],
                lhsT=words[v][:, c, :].bitcast(FP4X4),
                lhsT_scale=planes[v][:, c, :],
                rhs=codes[c][:].bitcast(FP8X4),
                rhs_scale=x_scales[c][:],
                start=(c == 0),
                stop=(c == PASSES - 1),
            )

        done = {v: 0 for v in convs}

        def multiply_up_to(v, c):
            for late in range(done[v], c + 1):
                multiply(v, late)
            done[v] = max(done[v], c + 1)

        def multiply_after_quantise(c):
            if c < PASSES - 1:
                multiply_up_to("theta", min(c - 2, PASSES - CHUNK - 1))
                multiply_up_to("phi", c - 1)
            else:
                multiply_up_to("theta", c - 1)
            multiply_up_to("g", c)
            if c >= PASSES - 2:
                multiply_up_to("phi", c)
            if c == PASSES - 1:
                multiply_up_to("theta", c)

        regroup(0)
        for c in range(PASSES):
            early = c + 1 < PASSES - TAIL
            if early:
                regroup(c + 1)
            quantise(c)
            multiply_after_quantise(c)
            if not early and c + 1 < PASSES:
                regroup(c + 1)

        pooled = {}
        for v in ("g", "phi"):
            pooled[v] = resident.tile([D, N // 4], F32, name="pooled_%s" % v)
            nc.vector.tensor_reduce(
                out=pooled[v][:].rearrange("d (a b) -> d a b", b=WIDTH // 2),
                in_=acc[v][:].rearrange("d (a e b f) -> d a b e f", e=2, b=WIDTH // 2, f=2),
                axis=mybir.AxisListType.XY,
                op=mybir.AluOpType.max,
            )
        theta = resident.tile([D, N], F32, name="theta")
        nc.scalar.activation(out=theta[:], in_=acc["theta"][:], func=IDENTITY, bias=bias["theta"][:])
        nc.sync.dma_start(out=out_1[0], in_=theta[:])
        for v, out in (("g", out_0), ("phi", out_2)):
            biased = resident.tile([D, N // 4], F32, name="biased_%s" % v)
            nc.scalar.activation(out=biased[:], in_=pooled[v][:], func=IDENTITY, bias=bias[v][:])
            nc.sync.dma_start(out=out[0], in_=biased[:])
